import numpy as np
import ml_dtypes


def mxq(x, axis, fmt="e4m3"):
    dtype, down = {"e4m3": (ml_dtypes.float8_e4m3fn, 7), "e5m2": (ml_dtypes.float8_e5m2, 14)}[fmt]
    v = np.moveaxis(np.asarray(x, np.float32).astype(ml_dtypes.bfloat16).astype(np.float64), axis, -1)
    blocks = v.reshape(v.shape[:-1] + (-1, 32))
    amax = np.abs(blocks).max(-1, keepdims=True)
    byte = np.maximum(np.where(amax > 0, np.frexp(amax)[1] - 1 + 127, 0) - down, 1)
    scale = np.exp2(byte - 127.0)
    codes = (blocks / scale).astype(np.float32).astype(dtype).astype(np.float64)
    return np.moveaxis((codes * scale).reshape(v.shape), -1, axis)


WIDE = False


def mx_kscale(k):
    if not WIDE:
        return np.ones(k)
    levels = np.array([20, -20, 10, -10, 0])
    a = np.random.permutation(np.resize(levels, k // 512 * 4)).reshape(k // 512, 4)
    idx = np.arange(k)
    return np.exp2(a[idx // 512, idx % 128 // 32])


BF16 = ml_dtypes.bfloat16


def bf(x):
    return np.asarray(x, np.float32).astype(BF16)


def f64(x):
    return np.asarray(x).astype(np.float64)


B, D_IN, D_OUT = 2048, 1024, 512
MASK_DENSITY = 0.25


def setup_inputs():
    u = mx_kscale(D_OUT)
    x0 = bf(np.random.standard_normal((B, D_IN)))
    x1 = bf(np.random.standard_normal((B, D_IN)))
    w0 = bf(np.random.standard_normal((D_OUT, D_IN)) * 2.0 / np.sqrt(D_IN) / u[:, None])
    w1 = bf(np.random.standard_normal((D_OUT, D_IN)) * 2.0 / np.sqrt(D_IN) / u[:, None])
    m0 = bf((np.random.random_sample((D_OUT, D_IN)) < MASK_DENSITY).astype(np.float64))
    m1 = bf((np.random.random_sample((D_OUT, D_IN)) < MASK_DENSITY).astype(np.float64))
    g = np.random.standard_normal((B, D_OUT)) * np.exp2(np.random.randint(-12, 1, (B, 1))) * 8.0 * u[None, :]
    return {"x0": x0, "x1": x1, "w0": w0, "w1": w1, "m0": m0, "m1": m1, "grad_out": bf(g)}


def reference(x0, x1, w0, w1, m0, m1, grad_out):
    wm0 = f64(w0) * f64(m0)
    return mxq(f64(grad_out), 1, "e5m2") @ mxq(wm0, 0, "e4m3")

@@ -1,0 +1,180 @@
+from contextlib import ExitStack
+
+import concourse.mybir as mybir
+from concourse.masks import make_identity
+
+F32 = mybir.dt.float32
+BF16 = mybir.dt.bfloat16
+U32 = mybir.dt.uint32
+U8 = mybir.dt.uint8
+E4M3X4 = mybir.dt.float8_e4m3fn_x4
+E5M2X4 = mybir.dt.float8_e5m2_x4
+
+P = 128
+TOKENS, D_IN, D_OUT = 2048, 1024, 512
+TILES = TOKENS // P
+HALF = 512
+FLOPS = 2 * TOKENS * D_IN * D_OUT
+BYTES = 2 * TOKENS * D_OUT + 2 * 2 * D_OUT * D_IN + 4 * TOKENS * D_IN
+PIN = True
+
+G_CHUNKS = ((0, 4), (4, 8), (8, 16))
+UNITS = ((0, 2, 0, 1), (2, 2, 0, 1), (0, 2, 1, 1), (2, 2, 1, 1), (4, 2, 0, 2), (6, 2, 0, 2), (8, 4, 0, 2), (12, 4, 0, 2))
+
+
+def tile_layer_t_kernel(tc, x0, x1, w0, w1, m0, m1, grad_out, out):
+    nc = tc.nc
+    w_rows = w0.rearrange("(p t) c -> p t c", t=4)
+    m_rows = m0.rearrange("(p t) c -> p t c", t=4)
+    g_rows = grad_out.rearrange("(p i) k -> p i k", i=TILES)
+    o_rows = out.rearrange("(p i) d -> p i d", i=TILES)
+
+    with ExitStack() as ctx:
+        keep = ctx.enter_context(tc.tile_pool(name="keep", bufs=1))
+        xt_pool = ctx.enter_context(tc.psum_pool(name="xt_pool", bufs=2))
+        acc_pool = ctx.enter_context(tc.psum_pool(name="acc_pool", bufs=6))
+        if PIN:
+            ctx.enter_context(tc.manual_schedule())
+
+        w_raw = [keep.tile([P, 4, HALF], BF16, name="w_raw%d" % h) for h in range(2)]
+        m_raw = [keep.tile([P, 4, HALF], BF16, name="m_raw%d" % h) for h in range(2)]
+        wm = [keep.tile([P, 4, HALF], BF16, name="wm%d" % h) for h in range(2)]
+        w_grp = [keep.tile([P, HALF, 4], BF16, name="w_grp%d" % h, align_bytes=64) for h in range(2)]
+        w_codes = [keep.tile([P, HALF], U32, name="w_codes%d" % h, align_bytes=64) for h in range(2)]
+        w_scales = [keep.tile([P, HALF], U8, name="w_scales%d" % h, align_bytes=64) for h in range(2)]
+        g_raw = [keep.tile([P, b - a, D_OUT], BF16, name="g_raw%d" % c) for c, (a, b) in enumerate(G_CHUNKS)]
+        g_grp = [keep.tile([P, 2 * HALF], BF16, name="g_grp%d" % j, align_bytes=64) for j in range(TILES // 2)]
+        g_codes = [keep.tile([P, 2 * P], U32, name="g_codes%d" % j, align_bytes=64) for j in range(TILES // 2)]
+        g_scales = [keep.tile([P, 2 * P], U8, name="g_scales%d" % j, align_bytes=64) for j in range(TILES // 2)]
+        o_sb = [keep.tile([P, n, nh * HALF], F32, name="o_sb%d" % s) for s, (a, n, h0, nh) in enumerate(UNITS)]
+        ident = keep.tile([P, P], F32, name="ident")
+
+        where_g = {}
+        for c, (a, b) in enumerate(G_CHUNKS):
+            for i in range(a, b):
+                where_g[i] = (c, i - a)
+        where_o = {}
+        for s, (a, n, h0, nh) in enumerate(UNITS):
+            for i in range(a, a + n):
+                for h in range(h0, h0 + nh):
+                    where_o[(i, h)] = (s, i - a, h - h0)
+
+        def load_w(h):
+            cols = slice(h * HALF, (h + 1) * HALF)
+            nc.sync.dma_start(out=w_raw[h][:], in_=w_rows[:, :, cols])
+            nc.sync.dma_start(out=m_raw[h][:], in_=m_rows[:, :, cols])
+
+        def load_g(c):
+            a, b = G_CHUNKS[c]
+            nc.sync.dma_start(out=g_raw[c][:], in_=g_rows[:, a:b, :])
+
+        def weights(h):
+            nc.vector.tensor_tensor(out=wm[h][:], in0=w_raw[h][:], in1=m_raw[h][:], op=mybir.AluOpType.mult)
+            nc.vector.tensor_copy(
+                out=w_grp[h][:].rearrange("p (c i) t -> p c t i", i=4),
+                in_=wm[h][:].rearrange("p t (c i) -> p c t i", i=4),
+            )
+            nc.vector.quantize_mx(
+                out=w_codes[h][:].bitcast(E4M3X4),
+                scales=w_scales[h][:],
+                in_=w_grp[h][:].rearrange("p c t -> p (c t)"),
+            )
+
+        xts = {}
+
+        def transposes(pair):
+            xt = xt_pool.tile([P, 2, 2, P], F32, name="xt")
+            for j in range(2):
+                c, row = where_g[2 * pair + j]
+                words = g_raw[c][:].bitcast(F32)[:, row, :].rearrange("p (q u) -> p u q", u=2)
+                for u in range(2):
+                    nc.tensor.transpose(xt[:, j, u, :], words[:, u, :], ident[:])
+            xts[pair] = xt
+
+        def copy_out(pair):
+            nc.scalar.copy(
+                out=g_grp[pair][:].bitcast(F32).rearrange("p (j r u) -> p j r u", j=2, u=2),
+                in_=xts[pair][:].rearrange("p j u r -> p j r u"),
+            )
+
+        def quantise(pair):
+            nc.vector.quantize_mx(
+                out=g_codes[pair][:].bitcast(E5M2X4), scales=g_scales[pair][:], in_=g_grp[pair][:]
+            )
+
+        def product(i, h, on_vector):
+            pair, j = divmod(i, 2)
+            toks = slice(j * P, (j + 1) * P)
+            acc = acc_pool.tile([P, HALF], F32, name="acc")
+            nc.tensor.matmul_mx(
+                out=acc[:],
+                lhsT=g_codes[pair][:, toks].bitcast(E5M2X4),
+                lhsT_scale=g_scales[pair][:, toks],
+                rhs=w_codes[h][:].bitcast(E4M3X4),
+                rhs_scale=w_scales[h][:],
+                start=True,
+                stop=True,
+            )
+            s, row, hh = where_o[(i, h)]
+            dst = o_sb[s][:, row, hh * HALF : (hh + 1) * HALF]
+            if on_vector:
+                nc.vector.tensor_copy(out=dst, in_=acc[:])
+            else:
+                nc.scalar.copy(out=dst, in_=acc[:])
+
+        def store(s):
+            a, n, h0, nh = UNITS[s]
+            nc.sync.dma_start(out=o_rows[:, a : a + n, h0 * HALF : (h0 + nh) * HALF], in_=o_sb[s][:])
+
+        load_w(0)
+        load_g(0)
+        load_w(1)
+        load_g(1)
+        load_g(2)
+        make_identity(nc, ident[:])
+
+        transposes(0)
+        transposes(1)
+        weights(0)
+        copy_out(0)
+        copy_out(1)
+        quantise(0)
+        quantise(1)
+
+        for i in range(4):
+            product(i, 0, False)
+            if i % 2 == 1:
+                store(i // 2)
+        transposes(2)
+        transposes(3)
+        weights(1)
+        copy_out(2)
+        copy_out(3)
+        quantise(2)
+
+        for i in range(4):
+            product(i, 1, i % 2 == 0)
+            if i % 2 == 1:
+                store(2 + i // 2)
+        quantise(3)
+        transposes(4)
+        transposes(5)
+
+        for pair in range(2, 8):
+            if pair + 2 < 8:
+                copy_out(pair + 2)
+            for i in (2 * pair, 2 * pair + 1):
+                product(i, 0, False)
+                product(i, 1, True)
+            if pair + 2 < 8:
+                quantise(pair + 2)
+            if pair == 2:
+                store(4)
+            if pair == 3:
+                store(5)
+                transposes(6)
+                transposes(7)
+            if pair == 5:
+                store(6)
+            if pair == 7:
+                store(7)

@@ -13,13 +13,21 @@ E5M2X4 = mybir.dt.float8_e5m2_x4
 P = 128
 TOKENS, D_IN, D_OUT = 2048, 1024, 512
 TILES = TOKENS // P
+PAIRS = TILES // 2
 HALF = 512
 FLOPS = 2 * TOKENS * D_IN * D_OUT
 BYTES = 2 * TOKENS * D_OUT + 2 * 2 * D_OUT * D_IN + 4 * TOKENS * D_IN
-PIN = True
 
-G_CHUNKS = ((0, 4), (4, 8), (8, 16))
-UNITS = ((0, 2, 0, 1), (2, 2, 0, 1), (0, 2, 1, 1), (2, 2, 1, 1), (4, 2, 0, 2), (6, 2, 0, 2), (8, 4, 0, 2), (12, 4, 0, 2))
+EARLY_PAIRS = 3
+EARLY = 2 * EARLY_PAIRS
+PAIR_STORES_FROM = 5
+G_CHUNKS = ((0, 2), (2, EARLY), (EARLY, TILES))
+UNITS = (
+    tuple((i, 1, 0, 1) for i in range(EARLY))
+    + ((0, 1, 1, 1), (1, 1, 1, 1), (2, 2, 1, 1), (4, 2, 1, 1))
+    + tuple((i, 1, 0, 2) for i in range(EARLY, 2 * PAIR_STORES_FROM))
+    + tuple((2 * j, 2, 0, 2) for j in range(PAIR_STORES_FROM, PAIRS))
+)
 
 
 def tile_layer_t_kernel(tc, x0, x1, w0, w1, m0, m1, grad_out, out):
@@ -31,21 +39,21 @@ def tile_layer_t_kernel(tc, x0, x1, w0, w1, m0, m1, grad_out, out):
 
     with ExitStack() as ctx:
         keep = ctx.enter_context(tc.tile_pool(name="keep", bufs=1))
-        xt_pool = ctx.enter_context(tc.psum_pool(name="xt_pool", bufs=2))
-        acc_pool = ctx.enter_context(tc.psum_pool(name="acc_pool", bufs=6))
-        if PIN:
-            ctx.enter_context(tc.manual_schedule())
+        xt_pool = ctx.enter_context(tc.psum_pool(name="xt_pool", bufs=3))
+        acc_pool = ctx.enter_context(tc.psum_pool(name="acc_pool", bufs=5))
+        ctx.enter_context(tc.manual_schedule())
 
-        w_raw = [keep.tile([P, 4, HALF], BF16, name="w_raw%d" % h) for h in range(2)]
-        m_raw = [keep.tile([P, 4, HALF], BF16, name="m_raw%d" % h) for h in range(2)]
+        pieces = (((0, 2), (2, 4)), ((0, 4),))
+        w_raw = [[keep.tile([P, b - a, HALF], BF16, name="w_raw%d_%d" % (h, a)) for a, b in pieces[h]] for h in range(2)]
+        m_raw = [[keep.tile([P, b - a, HALF], BF16, name="m_raw%d_%d" % (h, a)) for a, b in pieces[h]] for h in range(2)]
         wm = [keep.tile([P, 4, HALF], BF16, name="wm%d" % h) for h in range(2)]
         w_grp = [keep.tile([P, HALF, 4], BF16, name="w_grp%d" % h, align_bytes=64) for h in range(2)]
         w_codes = [keep.tile([P, HALF], U32, name="w_codes%d" % h, align_bytes=64) for h in range(2)]
         w_scales = [keep.tile([P, HALF], U8, name="w_scales%d" % h, align_bytes=64) for h in range(2)]
         g_raw = [keep.tile([P, b - a, D_OUT], BF16, name="g_raw%d" % c) for c, (a, b) in enumerate(G_CHUNKS)]
-        g_grp = [keep.tile([P, 2 * HALF], BF16, name="g_grp%d" % j, align_bytes=64) for j in range(TILES // 2)]
-        g_codes = [keep.tile([P, 2 * P], U32, name="g_codes%d" % j, align_bytes=64) for j in range(TILES // 2)]
-        g_scales = [keep.tile([P, 2 * P], U8, name="g_scales%d" % j, align_bytes=64) for j in range(TILES // 2)]
+        g_grp = [keep.tile([P, 2 * HALF], BF16, name="g_grp%d" % j, align_bytes=64) for j in range(PAIRS)]
+        g_codes = [keep.tile([P, 2 * P], U32, name="g_codes%d" % j, align_bytes=64) for j in range(PAIRS)]
+        g_scales = [keep.tile([P, 2 * P], U8, name="g_scales%d" % j, align_bytes=64) for j in range(PAIRS)]
         o_sb = [keep.tile([P, n, nh * HALF], F32, name="o_sb%d" % s) for s, (a, n, h0, nh) in enumerate(UNITS)]
         ident = keep.tile([P, P], F32, name="ident")
 
@@ -54,26 +62,34 @@ def tile_layer_t_kernel(tc, x0, x1, w0, w1, m0, m1, grad_out, out):
             for i in range(a, b):
                 where_g[i] = (c, i - a)
         where_o = {}
+        banks_left = {}
         for s, (a, n, h0, nh) in enumerate(UNITS):
+            banks_left[s] = n * nh
             for i in range(a, a + n):
                 for h in range(h0, h0 + nh):
                     where_o[(i, h)] = (s, i - a, h - h0)
 
         def load_w(h):
             cols = slice(h * HALF, (h + 1) * HALF)
-            nc.sync.dma_start(out=w_raw[h][:], in_=w_rows[:, :, cols])
-            nc.sync.dma_start(out=m_raw[h][:], in_=m_rows[:, :, cols])
+            for q, (a, b) in enumerate(pieces[h]):
+                nc.sync.dma_start(out=w_raw[h][q][:], in_=w_rows[:, a:b, cols])
+                nc.sync.dma_start(out=m_raw[h][q][:], in_=m_rows[:, a:b, cols])
 
         def load_g(c):
             a, b = G_CHUNKS[c]
             nc.sync.dma_start(out=g_raw[c][:], in_=g_rows[:, a:b, :])
 
-        def weights(h):
-            nc.vector.tensor_tensor(out=wm[h][:], in0=w_raw[h][:], in1=m_raw[h][:], op=mybir.AluOpType.mult)
+        def mask(h):
+            for q, (a, b) in enumerate(pieces[h]):
+                nc.vector.tensor_tensor(out=wm[h][:, a:b, :], in0=w_raw[h][q][:], in1=m_raw[h][q][:], op=mybir.AluOpType.mult)
+
+        def interleave(h):
             nc.vector.tensor_copy(
                 out=w_grp[h][:].rearrange("p (c i) t -> p c t i", i=4),
                 in_=wm[h][:].rearrange("p t (c i) -> p c t i", i=4),
             )
+
+        def quantise_w(h):
             nc.vector.quantize_mx(
                 out=w_codes[h][:].bitcast(E4M3X4),
                 scales=w_scales[h][:],
@@ -121,60 +137,53 @@ def tile_layer_t_kernel(tc, x0, x1, w0, w1, m0, m1, grad_out, out):
                 nc.vector.tensor_copy(out=dst, in_=acc[:])
             else:
                 nc.scalar.copy(out=dst, in_=acc[:])
-
-        def store(s):
-            a, n, h0, nh = UNITS[s]
-            nc.sync.dma_start(out=o_rows[:, a : a + n, h0 * HALF : (h0 + nh) * HALF], in_=o_sb[s][:])
+            banks_left[s] -= 1
+            if banks_left[s] == 0:
+                a, n, h0, nh = UNITS[s]
+                nc.sync.dma_start(out=o_rows[:, a : a + n, h0 * HALF : (h0 + nh) * HALF], in_=o_sb[s][:])
 
         load_w(0)
         load_g(0)
-        load_w(1)
         load_g(1)
+        load_w(1)
         load_g(2)
         make_identity(nc, ident[:])
 
-        transposes(0)
-        transposes(1)
-        weights(0)
-        copy_out(0)
-        copy_out(1)
-        quantise(0)
-        quantise(1)
-
-        for i in range(4):
+        mask(0)
+        interleave(0)
+        for pair in range(EARLY_PAIRS):
+            transposes(pair)
+            copy_out(pair)
+        quantise_w(0)
+        for pair in range(EARLY_PAIRS):
+            quantise(pair)
+        mask(1)
+        for i in range(EARLY):
             product(i, 0, False)
-            if i % 2 == 1:
-                store(i // 2)
-        transposes(2)
+        interleave(1)
+        quantise_w(1)
         transposes(3)
-        weights(1)
-        copy_out(2)
         copy_out(3)
-        quantise(2)
-
-        for i in range(4):
-            product(i, 1, i % 2 == 0)
-            if i % 2 == 1:
-                store(2 + i // 2)
+        product(0, 1, True)
+        product(1, 1, False)
         quantise(3)
         transposes(4)
-        transposes(5)
+        product(2, 1, True)
+        product(3, 1, False)
+        copy_out(4)
+        product(4, 1, True)
+        product(5, 1, False)
+        quantise(4)
 
-        for pair in range(2, 8):
-            if pair + 2 < 8:
-                copy_out(pair + 2)
-            for i in (2 * pair, 2 * pair + 1):
-                product(i, 0, False)
-                product(i, 1, True)
-            if pair + 2 < 8:
-                quantise(pair + 2)
-            if pair == 2:
-                store(4)
-            if pair == 3:
-                store(5)
-                transposes(6)
-                transposes(7)
-            if pair == 5:
-                store(6)
-            if pair == 7:
-                store(7)
+        for pair in range(EARLY_PAIRS, PAIRS):
+            ahead = pair + 2
+            if ahead < PAIRS:
+                transposes(ahead)
+            product(2 * pair, 0, False)
+            product(2 * pair, 1, True)
+            if ahead < PAIRS:
+                copy_out(ahead)
+            product(2 * pair + 1, 0, False)
+            product(2 * pair + 1, 1, True)
+            if ahead < PAIRS:
+                quantise(ahead)

@@ -107,11 +107,13 @@ def tile_layer_t_kernel(tc, x0, x1, w0, w1, m0, m1, grad_out, out):
                     nc.tensor.transpose(xt[:, j, u, :], words[:, u, :], ident[:])
             xts[pair] = xt
 
-        def copy_out(pair):
-            nc.scalar.copy(
-                out=g_grp[pair][:].bitcast(F32).rearrange("p (j r u) -> p j r u", j=2, u=2),
-                in_=xts[pair][:].rearrange("p j u r -> p j r u"),
-            )
+        def copy_out(pair, on_vector=False):
+            dst = g_grp[pair][:].bitcast(F32).rearrange("p (j r u) -> p j r u", j=2, u=2)
+            src = xts[pair][:].rearrange("p j u r -> p j r u")
+            if on_vector:
+                nc.vector.tensor_copy(out=dst, in_=src)
+            else:
+                nc.scalar.copy(out=dst, in_=src)
 
         def quantise(pair):
             nc.vector.quantize_mx(
@@ -155,25 +157,26 @@ def tile_layer_t_kernel(tc, x0, x1, w0, w1, m0, m1, grad_out, out):
             transposes(pair)
             copy_out(pair)
         quantise_w(0)
-        for pair in range(EARLY_PAIRS):
-            quantise(pair)
+        quantise(0)
+        quantise(1)
         mask(1)
+        quantise(2)
         for i in range(EARLY):
             product(i, 0, False)
         interleave(1)
         quantise_w(1)
         transposes(3)
-        copy_out(3)
-        product(0, 1, True)
-        product(1, 1, False)
-        quantise(3)
         transposes(4)
-        product(2, 1, True)
-        product(3, 1, False)
+        copy_out(3, True)
+        quantise(3)
         copy_out(4)
-        product(4, 1, True)
-        product(5, 1, False)
+        product(0, 1, False)
+        product(1, 1, True)
+        product(2, 1, False)
+        product(3, 1, True)
         quantise(4)
+        product(4, 1, False)
+        product(5, 1, True)
 
         for pair in range(EARLY_PAIRS, PAIRS):
             ahead = pair + 2

@@ -20,13 +20,12 @@ BYTES = 2 * TOKENS * D_OUT + 2 * 2 * D_OUT * D_IN + 4 * TOKENS * D_IN
 
 EARLY_PAIRS = 3
 EARLY = 2 * EARLY_PAIRS
-PAIR_STORES_FROM = 5
+LATE_STORES = ((6, 2), (8, 2), (10, 4), (14, 2))
 G_CHUNKS = ((0, 2), (2, EARLY), (EARLY, TILES))
 UNITS = (
     tuple((i, 1, 0, 1) for i in range(EARLY))
     + ((0, 1, 1, 1), (1, 1, 1, 1), (2, 2, 1, 1), (4, 2, 1, 1))
-    + tuple((i, 1, 0, 2) for i in range(EARLY, 2 * PAIR_STORES_FROM))
-    + tuple((2 * j, 2, 0, 2) for j in range(PAIR_STORES_FROM, PAIRS))
+    + tuple((a, n, 0, 2) for a, n in LATE_STORES)
 )
 
 

@@ -21,7 +21,7 @@ BYTES = 2 * TOKENS * D_OUT + 2 * 2 * D_OUT * D_IN + 4 * TOKENS * D_IN
 EARLY_PAIRS = 3
 EARLY = 2 * EARLY_PAIRS
 LATE_STORES = ((6, 2), (8, 2), (10, 4), (14, 2))
-G_CHUNKS = ((0, 2), (2, EARLY), (EARLY, TILES))
+G_CHUNKS = ((0, 2), (2, EARLY), (EARLY, EARLY + 4), (EARLY + 4, TILES))
 UNITS = (
     tuple((i, 1, 0, 1) for i in range(EARLY))
     + ((0, 1, 1, 1), (1, 1, 1, 1), (2, 2, 1, 1), (4, 2, 1, 1))
@@ -42,7 +42,7 @@ def tile_layer_t_kernel(tc, x0, x1, w0, w1, m0, m1, grad_out, out):
         acc_pool = ctx.enter_context(tc.psum_pool(name="acc_pool", bufs=5))
         ctx.enter_context(tc.manual_schedule())
 
-        pieces = (((0, 2), (2, 4)), ((0, 4),))
+        pieces = (((0, 2), (2, 3), (3, 4)), ((0, 2), (2, 4)))
         w_raw = [[keep.tile([P, b - a, HALF], BF16, name="w_raw%d_%d" % (h, a)) for a, b in pieces[h]] for h in range(2)]
         m_raw = [[keep.tile([P, b - a, HALF], BF16, name="m_raw%d_%d" % (h, a)) for a, b in pieces[h]] for h in range(2)]
         wm = [keep.tile([P, 4, HALF], BF16, name="wm%d" % h) for h in range(2)]
@@ -78,9 +78,9 @@ def tile_layer_t_kernel(tc, x0, x1, w0, w1, m0, m1, grad_out, out):
             a, b = G_CHUNKS[c]
             nc.sync.dma_start(out=g_raw[c][:], in_=g_rows[:, a:b, :])
 
-        def mask(h):
-            for q, (a, b) in enumerate(pieces[h]):
-                nc.vector.tensor_tensor(out=wm[h][:, a:b, :], in0=w_raw[h][q][:], in1=m_raw[h][q][:], op=mybir.AluOpType.mult)
+        def mask(h, q):
+            a, b = pieces[h][q]
+            nc.vector.tensor_tensor(out=wm[h][:, a:b, :], in0=w_raw[h][q][:], in1=m_raw[h][q][:], op=mybir.AluOpType.mult)
 
         def interleave(h):
             nc.vector.tensor_copy(
@@ -148,17 +148,20 @@ def tile_layer_t_kernel(tc, x0, x1, w0, w1, m0, m1, grad_out, out):
         load_g(1)
         load_w(1)
         load_g(2)
+        load_g(3)
         make_identity(nc, ident[:])
 
-        mask(0)
+        for q in range(3):
+            mask(0, q)
         interleave(0)
         for pair in range(EARLY_PAIRS):
             transposes(pair)
             copy_out(pair)
         quantise_w(0)
         quantise(0)
+        mask(1, 0)
         quantise(1)
-        mask(1)
+        mask(1, 1)
         quantise(2)
         for i in range(EARLY):
             product(i, 0, False)
@@ -168,14 +171,14 @@ def tile_layer_t_kernel(tc, x0, x1, w0, w1, m0, m1, grad_out, out):
         transposes(4)
         copy_out(3, True)
         quantise(3)
-        copy_out(4)
         product(0, 1, False)
         product(1, 1, True)
         product(2, 1, False)
+        copy_out(4)
         product(3, 1, True)
-        quantise(4)
         product(4, 1, False)
         product(5, 1, True)
+        quantise(4)
 
         for pair in range(EARLY_PAIRS, PAIRS):
             ahead = pair + 2

from contextlib import ExitStack

import concourse.mybir as mybir
from concourse.masks import make_identity

F32 = mybir.dt.float32
BF16 = mybir.dt.bfloat16
U32 = mybir.dt.uint32
U8 = mybir.dt.uint8
E4M3X4 = mybir.dt.float8_e4m3fn_x4
E5M2X4 = mybir.dt.float8_e5m2_x4

P = 128
TOKENS, D_IN, D_OUT = 2048, 1024, 512
TILES = TOKENS // P
PAIRS = TILES // 2
HALF = 512
FLOPS = 2 * TOKENS * D_IN * D_OUT
BYTES = 2 * TOKENS * D_OUT + 2 * 2 * D_OUT * D_IN + 4 * TOKENS * D_IN

EARLY_PAIRS = 3
EARLY = 2 * EARLY_PAIRS
LATE_STORES = ((6, 2), (8, 2), (10, 4), (14, 2))
G_CHUNKS = ((0, 2), (2, EARLY), (EARLY, EARLY + 4), (EARLY + 4, TILES))
UNITS = (
    tuple((i, 1, 0, 1) for i in range(EARLY))
    + ((0, 1, 1, 1), (1, 1, 1, 1), (2, 2, 1, 1), (4, 2, 1, 1))
    + tuple((a, n, 0, 2) for a, n in LATE_STORES)
)


def tile_layer_t_kernel(tc, x0, x1, w0, w1, m0, m1, grad_out, out):
    nc = tc.nc
    w_rows = w0.rearrange("(p t) c -> p t c", t=4)
    m_rows = m0.rearrange("(p t) c -> p t c", t=4)
    g_rows = grad_out.rearrange("(p i) k -> p i k", i=TILES)
    o_rows = out.rearrange("(p i) d -> p i d", i=TILES)

    with ExitStack() as ctx:
        keep = ctx.enter_context(tc.tile_pool(name="keep", bufs=1))
        xt_pool = ctx.enter_context(tc.psum_pool(name="xt_pool", bufs=3))
        acc_pool = ctx.enter_context(tc.psum_pool(name="acc_pool", bufs=5))
        ctx.enter_context(tc.manual_schedule())

        pieces = (((0, 2), (2, 3), (3, 4)), ((0, 2), (2, 4)))
        w_raw = [[keep.tile([P, b - a, HALF], BF16, name="w_raw%d_%d" % (h, a)) for a, b in pieces[h]] for h in range(2)]
        m_raw = [[keep.tile([P, b - a, HALF], BF16, name="m_raw%d_%d" % (h, a)) for a, b in pieces[h]] for h in range(2)]
        wm = [keep.tile([P, 4, HALF], BF16, name="wm%d" % h) for h in range(2)]
        w_grp = [keep.tile([P, HALF, 4], BF16, name="w_grp%d" % h, align_bytes=64) for h in range(2)]
        w_codes = [keep.tile([P, HALF], U32, name="w_codes%d" % h, align_bytes=64) for h in range(2)]
        w_scales = [keep.tile([P, HALF], U8, name="w_scales%d" % h, align_bytes=64) for h in range(2)]
        g_raw = [keep.tile([P, b - a, D_OUT], BF16, name="g_raw%d" % c) for c, (a, b) in enumerate(G_CHUNKS)]
        g_grp = [keep.tile([P, 2 * HALF], BF16, name="g_grp%d" % j, align_bytes=64) for j in range(PAIRS)]
        g_codes = [keep.tile([P, 2 * P], U32, name="g_codes%d" % j, align_bytes=64) for j in range(PAIRS)]
        g_scales = [keep.tile([P, 2 * P], U8, name="g_scales%d" % j, align_bytes=64) for j in range(PAIRS)]
        o_sb = [keep.tile([P, n, nh * HALF], F32, name="o_sb%d" % s) for s, (a, n, h0, nh) in enumerate(UNITS)]
        ident = keep.tile([P, P], F32, name="ident")

        where_g = {}
        for c, (a, b) in enumerate(G_CHUNKS):
            for i in range(a, b):
                where_g[i] = (c, i - a)
        where_o = {}
        banks_left = {}
        for s, (a, n, h0, nh) in enumerate(UNITS):
            banks_left[s] = n * nh
            for i in range(a, a + n):
                for h in range(h0, h0 + nh):
                    where_o[(i, h)] = (s, i - a, h - h0)

        def load_w(h):
            cols = slice(h * HALF, (h + 1) * HALF)
            for q, (a, b) in enumerate(pieces[h]):
                nc.sync.dma_start(out=w_raw[h][q][:], in_=w_rows[:, a:b, cols])
                nc.sync.dma_start(out=m_raw[h][q][:], in_=m_rows[:, a:b, cols])

        def load_g(c):
            a, b = G_CHUNKS[c]
            nc.sync.dma_start(out=g_raw[c][:], in_=g_rows[:, a:b, :])

        def mask(h, q):
            a, b = pieces[h][q]
            nc.vector.tensor_tensor(out=wm[h][:, a:b, :], in0=w_raw[h][q][:], in1=m_raw[h][q][:], op=mybir.AluOpType.mult)

        def interleave(h):
            nc.vector.tensor_copy(
                out=w_grp[h][:].rearrange("p (c i) t -> p c t i", i=4),
                in_=wm[h][:].rearrange("p t (c i) -> p c t i", i=4),
            )

        def quantise_w(h):
            nc.vector.quantize_mx(
                out=w_codes[h][:].bitcast(E4M3X4),
                scales=w_scales[h][:],
                in_=w_grp[h][:].rearrange("p c t -> p (c t)"),
            )

        xts = {}

        def transposes(pair):
            xt = xt_pool.tile([P, 2, 2, P], F32, name="xt")
            for j in range(2):
                c, row = where_g[2 * pair + j]
                words = g_raw[c][:].bitcast(F32)[:, row, :].rearrange("p (q u) -> p u q", u=2)
                for u in range(2):
                    nc.tensor.transpose(xt[:, j, u, :], words[:, u, :], ident[:])
            xts[pair] = xt

        def copy_out(pair, on_vector=False):
            dst = g_grp[pair][:].bitcast(F32).rearrange("p (j r u) -> p j r u", j=2, u=2)
            src = xts[pair][:].rearrange("p j u r -> p j r u")
            if on_vector:
                nc.vector.tensor_copy(out=dst, in_=src)
            else:
                nc.scalar.copy(out=dst, in_=src)

        def quantise(pair):
            nc.vector.quantize_mx(
                out=g_codes[pair][:].bitcast(E5M2X4), scales=g_scales[pair][:], in_=g_grp[pair][:]
            )

        def product(i, h, on_vector):
            pair, j = divmod(i, 2)
            toks = slice(j * P, (j + 1) * P)
            acc = acc_pool.tile([P, HALF], F32, name="acc")
            nc.tensor.matmul_mx(
                out=acc[:],
                lhsT=g_codes[pair][:, toks].bitcast(E5M2X4),
                lhsT_scale=g_scales[pair][:, toks],
                rhs=w_codes[h][:].bitcast(E4M3X4),
                rhs_scale=w_scales[h][:],
                start=True,
                stop=True,
            )
            s, row, hh = where_o[(i, h)]
            dst = o_sb[s][:, row, hh * HALF : (hh + 1) * HALF]
            if on_vector:
                nc.vector.tensor_copy(out=dst, in_=acc[:])
            else:
                nc.scalar.copy(out=dst, in_=acc[:])
            banks_left[s] -= 1
            if banks_left[s] == 0:
                a, n, h0, nh = UNITS[s]
                nc.sync.dma_start(out=o_rows[:, a : a + n, h0 * HALF : (h0 + nh) * HALF], in_=o_sb[s][:])

        load_w(0)
        load_g(0)
        load_g(1)
        load_w(1)
        load_g(2)
        load_g(3)
        make_identity(nc, ident[:])

        for q in range(3):
            mask(0, q)
        interleave(0)
        for pair in range(EARLY_PAIRS):
            transposes(pair)
            copy_out(pair)
        quantise_w(0)
        quantise(0)
        mask(1, 0)
        quantise(1)
        mask(1, 1)
        quantise(2)
        for i in range(EARLY):
            product(i, 0, False)
        interleave(1)
        quantise_w(1)
        transposes(3)
        transposes(4)
        copy_out(3, True)
        quantise(3)
        product(0, 1, False)
        product(1, 1, True)
        product(2, 1, False)
        copy_out(4)
        product(3, 1, True)
        product(4, 1, False)
        product(5, 1, True)
        quantise(4)

        for pair in range(EARLY_PAIRS, PAIRS):
            ahead = pair + 2
            if ahead < PAIRS:
                transposes(ahead)
            product(2 * pair, 0, False)
            product(2 * pair, 1, True)
            if ahead < PAIRS:
                copy_out(ahead)
            product(2 * pair + 1, 0, False)
            product(2 * pair + 1, 1, True)
            if ahead < PAIRS:
                quantise(ahead)
